import numpy as np
import ml_dtypes


def mxq(x, axis, fmt="e4m3"):
    dtype, down = {"e4m3": (ml_dtypes.float8_e4m3fn, 7), "e5m2": (ml_dtypes.float8_e5m2, 14)}[fmt]
    v = np.moveaxis(np.asarray(x, np.float32).astype(ml_dtypes.bfloat16).astype(np.float64), axis, -1)
    blocks = v.reshape(v.shape[:-1] + (-1, 32))
    amax = np.abs(blocks).max(-1, keepdims=True)
    byte = np.maximum(np.where(amax > 0, np.frexp(amax)[1] - 1 + 127, 0) - down, 1)
    scale = np.exp2(byte - 127.0)
    codes = (blocks / scale).astype(np.float32).astype(dtype).astype(np.float64)
    return np.moveaxis((codes * scale).reshape(v.shape), -1, axis)


WIDE = False


def mx_kscale(k):
    if not WIDE:
        return np.ones(k)
    levels = np.array([10, -10, 5, -5, 0])
    a = np.random.permutation(np.resize(levels, k // 512 * 4)).reshape(k // 512, 4)
    idx = np.arange(k)
    return np.exp2(a[idx // 512, idx % 128 // 32])


BF16 = ml_dtypes.bfloat16


def bf(x):
    return np.asarray(x, np.float32).astype(BF16)


def f64(x):
    return np.asarray(x).astype(np.float64)


B, S, I, O = 4, 1024, 1024, 512


def softplus(v):
    return np.logaddexp(v, 0.0)


def setup_inputs():
    s = mx_kscale(I)
    bound = 7.0 / np.sqrt(I)
    return {"x": bf(np.random.standard_normal((B, S, I)) * s),
            "mu_weight": bf(np.random.uniform(-bound, bound, (O, I)) / s[None, :]),
            "sigma_weight": bf(1.0 + np.random.standard_normal((O, I))),
            "gate_param": bf(-0.1 + 0.1 * np.random.standard_normal(O)),
            "mu_bias": bf(0.1 * np.random.standard_normal(O))}


def reference(x, mu_weight, sigma_weight, gate_param, mu_bias):
    x = f64(x)
    mu = f64(mu_weight)
    orig_shape = x.shape
    xr = x.reshape(-1, mu.shape[1])
    keys = mu * softplus(f64(sigma_weight))
    scale = 1.0 / np.sqrt(mu.shape[1])
    xq = mxq(xr, 1, "e4m3")
    scores = (xq @ mxq(keys, 1, "e4m3").T) * scale
    raw_weights = np.maximum(scores - f64(gate_param)[None, :], 0.0)
    dense = xq @ mxq(mu, 1, "e4m3").T
    masked_output = dense * raw_weights + f64(mu_bias)[None, :]
    final_output = masked_output.reshape(*orig_shape[:-1], mu.shape[0])
    return (final_output, scores, masked_output)

@@ -1,0 +1,237 @@
+from contextlib import ExitStack
+
+import concourse.mybir as mybir
+from concourse.masks import make_identity
+
+F32 = mybir.dt.float32
+BF16 = mybir.dt.bfloat16
+U32 = mybir.dt.uint32
+U8 = mybir.dt.uint8
+FP8X4 = mybir.dt.float8_e4m3fn_x4
+ALU = mybir.AluOpType
+ACT = mybir.ActivationFunctionType
+
+P = 128
+ROWS = 4096
+K = 1024
+O = 512
+T = 4
+NCH = ROWS // (P * T)
+NPAIR = ROWS // (2 * P)
+NJ = O // P
+SCALE = 1.0 / 32.0
+CLAMP = 32.0
+LOOKAHEAD = 2
+FLUSH_AFTER = (1, 3, 7, 11, 15, 19, 23, 27, 29, 30, 31)
+
+FLOPS = 2 * 2 * ROWS * K * O
+
+
+def tile_sparsebayesianlinear_t_kernel(
+    tc, x, mu_weight, sigma_weight, gate_param, mu_bias, out_0, out_1, out_2
+):
+    nc = tc.nc
+    xv = x.flatten_outer_dims().rearrange("(c p t) k -> c p t k", c=NCH, p=P)
+    ov0 = out_0.flatten_outer_dims().rearrange("(c p t) o -> c p t o", c=NCH, p=P)
+    ov1 = out_1.rearrange("(c p t) o -> c p t o", c=NCH, p=P)
+    ov2 = out_2.rearrange("(c p t) o -> c p t o", c=NCH, p=P)
+
+    with ExitStack() as ctx:
+        const = ctx.enter_context(tc.tile_pool(name="const", bufs=1))
+        wts = ctx.enter_context(tc.tile_pool(name="wts", bufs=1))
+        xin = ctx.enter_context(tc.tile_pool(name="xin", bufs=1))
+        xgp = ctx.enter_context(tc.tile_pool(name="xgp", bufs=3))
+        xcp = ctx.enter_context(tc.tile_pool(name="xcp", bufs=6))
+        scp = ctx.enter_context(tc.tile_pool(name="scp", bufs=3))
+        mkp = ctx.enter_context(tc.tile_pool(name="mkp", bufs=3))
+        ttp = ctx.enter_context(tc.tile_pool(name="ttp", bufs=2))
+        mmp = ctx.enter_context(tc.tile_pool(name="mmp", bufs=3))
+        psg = ctx.enter_context(tc.psum_pool(name="psg", bufs=1))
+        psx = ctx.enter_context(tc.psum_pool(name="psx", bufs=2))
+        pss = ctx.enter_context(tc.psum_pool(name="pss", bufs=2))
+        psd = ctx.enter_context(tc.psum_pool(name="psd", bufs=3))
+
+        ident = const.tile([P, P], F32, name="ident")
+        make_identity(nc, ident[:])
+        ones = const.tile([P, P], BF16, name="ones")
+        nc.vector.memset(ones[:], 1.0)
+        vecs = const.tile([P, 2 * O], BF16, name="vecs")
+        nc.vector.memset(vecs[:], 0.0)
+        nc.scalar.dma_start(out=vecs[0:1, 0:O], in_=gate_param.unsqueeze(0))
+        nc.scalar.dma_start(out=vecs[0:1, O : 2 * O], in_=mu_bias.unsqueeze(0))
+        bias_sb = const.tile([P, O], F32, name="bias_sb")
+
+        sig = wts.tile([P, NJ * K], BF16, name="sig")
+        mur = wts.tile([P, NJ * K], BF16, name="mur")
+        vcl = wts.tile([P, NJ * K], BF16, name="vcl")
+        elog = wts.tile([P, NJ * K], F32, name="elog")
+        mu_g = wts.tile([P, 2 * O * 4], BF16, name="mu_g", align_bytes=64)
+        keys_g = wts.tile([P, 2 * O * 4], BF16, name="keys_g", align_bytes=64)
+        wc = wts.tile([P, 2 * 2 * O], U32, name="wc", align_bytes=64)
+        ws = wts.tile([P, 2 * 2 * O], U8, name="ws", align_bytes=64)
+
+        for j in range(NJ):
+            nc.sync.dma_start(out=sig[:, j * K : (j + 1) * K], in_=sigma_weight[j * P : (j + 1) * P, :])
+            nc.sync.dma_start(out=mur[:, j * K : (j + 1) * K], in_=mu_weight[j * P : (j + 1) * P, :])
+        x_sb = []
+        for c in range(NCH):
+            xt = xin.tile([P, T * K], BF16, name="x%d" % c)
+            nc.sync.dma_start(out=xt[:].rearrange("p (t k) -> p t k", t=T), in_=xv[c])
+            x_sb.append(xt)
+
+        def transpose_words(src32, col0, bank):
+            for i in range(4):
+                nc.tensor.transpose(
+                    out=bank[:, i * P : (i + 1) * P],
+                    in_=src32[:, col0 + i * P : col0 + (i + 1) * P],
+                    identity=ident[:],
+                )
+
+        vcl32 = vcl[:].bitcast(F32)
+        sig32 = sig[:].bitcast(F32)
+        mur32 = mur[:].bitcast(F32)
+        vc_pools = (pss, pss, psd, psd)
+        for j in range(NJ):
+            js = slice(j * K, (j + 1) * K)
+            nc.vector.tensor_scalar_min(out=vcl[:, js], in0=sig[:, js], scalar1=CLAMP)
+            bank = vc_pools[j].tile([P, O], F32, name="bk")
+            transpose_words(vcl32, j * (K // 2), bank)
+            nc.scalar.activation(out=elog[:, js], in_=bank[:].bitcast(BF16), func=ACT.Exp)
+
+        gate_ps = psg.tile([P, O], F32, name="gate_ps")
+        nc.tensor.matmul(out=gate_ps[:], lhsT=ones[:], rhs=vecs[:, 0:O], start=True, stop=True)
+        bias_ps = psx.tile([P, O], F32, name="bk")
+        nc.tensor.matmul(out=bias_ps[:], lhsT=ones[:], rhs=vecs[:, O : 2 * O], start=True, stop=True)
+
+        for j in range(NJ):
+            js = slice(j * K, (j + 1) * K)
+            nc.vector.tensor_scalar(
+                out=sig[:, js], in0=sig[:, js], scalar1=1.0 / CLAMP, scalar2=1.0, op0=ALU.mult, op1=ALU.max
+            )
+        nc.vector.tensor_copy(out=bias_sb[:], in_=bias_ps[:])
+        for j in range(NJ):
+            js = slice(j * K, (j + 1) * K)
+            nc.vector.tensor_tensor(out=sig[:, js], in0=sig[:, js], in1=mur[:, js], op=ALU.mult)
+
+        mu_g32 = mu_g[:].bitcast(F32).rearrange("p (g o u) -> p g o u", g=2, u=2)
+        mu_pools = (psd, psx, psx, psx)
+        for j in range(NJ):
+            bank = mu_pools[j].tile([P, O], F32, name="bk")
+            transpose_words(mur32, j * (K // 2), bank)
+            nc.vector.tensor_copy(
+                out=mu_g32[:, :, j * P : (j + 1) * P, :],
+                in_=bank[:].rearrange("p (g u r) -> p g r u", g=2, u=2),
+            )
+        for g in range(2):
+            nc.vector.quantize_mx(
+                out=wc[:, g * O : (g + 1) * O].bitcast(FP8X4),
+                scales=ws[:, g * O : (g + 1) * O],
+                in_=mu_g[:, g * 4 * O : (g + 1) * 4 * O],
+            )
+        m2_pools = (pss, pss, psd, psd)
+        m2_banks = []
+        for j in range(NJ):
+            bank = m2_pools[j].tile([P, O], F32, name="bk")
+            transpose_words(sig32, j * (K // 2), bank)
+            m2_banks.append(bank)
+
+        for j in range(NJ):
+            js = slice(j * K, (j + 1) * K)
+            nc.scalar.activation(out=elog[:, js], in_=elog[:, js], func=ACT.Ln, bias=1.0)
+            m2v = m2_banks[j][:].bitcast(BF16)
+            for g in range(2):
+                nc.vector.tensor_tensor(
+                    out=keys_g[:, g * 4 * O + j * 4 * P : g * 4 * O + (j + 1) * 4 * P].rearrange(
+                        "p (r u e) -> p r u e", u=2, e=2
+                    ),
+                    in0=elog[:, j * K + g * 512 : j * K + (g + 1) * 512].rearrange(
+                        "p (u r e) -> p r u e", u=2, e=2
+                    ),
+                    in1=m2v[:, g * 512 : (g + 1) * 512].rearrange("p (u r e) -> p r u e", u=2, e=2),
+                    op=ALU.mult,
+                )
+            for g in range(2):
+                w0 = 2 * O + g * O + j * P
+                nc.vector.quantize_mx(
+                    out=wc[:, w0 : w0 + P].bitcast(FP8X4),
+                    scales=ws[:, w0 : w0 + P],
+                    in_=keys_g[:, g * 4 * O + j * 4 * P : g * 4 * O + (j + 1) * 4 * P],
+                )
+
+        def prep(q):
+            c = q // 2
+            t0 = (q % 2) * 2
+            x32 = x_sb[c][:].bitcast(F32)
+            xg = xgp.tile([P, 2 * K], BF16, name="xg", align_bytes=64)
+            xg32 = xg[:].bitcast(F32).rearrange("p (a g r u) -> p a g r u", a=2, g=2, u=2)
+            banks = []
+            for a in range(2):
+                bank = psx.tile([P, O], F32, name="bk")
+                transpose_words(x32, (t0 + a) * (K // 2), bank)
+                banks.append(bank)
+            for a in range(2):
+                nc.scalar.copy(
+                    out=xg32[:, a], in_=banks[a][:].rearrange("p (g u r) -> p g r u", g=2, u=2)
+                )
+            xc = xcp.tile([P, 2 * 2 * P], U32, name="xc", align_bytes=64)
+            xs = xcp.tile([P, 2 * 2 * P], U8, name="xs", align_bytes=64)
+            nc.vector.quantize_mx(out=xc[:].bitcast(FP8X4), scales=xs[:], in_=xg[:])
+            return xc, xs
+
+        codes = {}
+        for q in range(LOOKAHEAD):
+            codes[q] = prep(q)
+
+        outs = {}
+        for q in range(NPAIR):
+            if q + LOOKAHEAD < NPAIR:
+                codes[q + LOOKAHEAD] = prep(q + LOOKAHEAD)
+            xc, xs = codes[q]
+            acc = []
+            for a in range(2):
+                d_ps = psd.tile([P, O], F32, name="bk")
+                s_ps = pss.tile([P, O], F32, name="bk")
+                for g in range(2):
+                    l0 = a * 2 * P + g * P
+                    for w, ps in ((0, d_ps), (1, s_ps)):
+                        w0 = w * 2 * O + g * O
+                        nc.tensor.matmul_mx(
+                            out=ps[:],
+                            lhsT=xc[:, l0 : l0 + P].bitcast(FP8X4),
+                            lhsT_scale=xs[:, l0 : l0 + P],
+                            rhs=wc[:, w0 : w0 + O].bitcast(FP8X4),
+                            rhs_scale=ws[:, w0 : w0 + O],
+                            start=(g == 0),
+                            stop=(g == 1),
+                        )
+                acc.append((s_ps, d_ps))
+            for a in range(2):
+                i = 2 * q + a
+                c = i // T
+                t = i % T
+                if t == 0:
+                    sc_new = scp.tile([P, T * O], F32, name="sc")
+                    mk_new = mkp.tile([P, T * O], F32, name="mk")
+                    outs["sc"] = sc_new
+                    outs["mk"] = mk_new
+                    outs["lo"] = 0
+                sc = outs["sc"]
+                mk = outs["mk"]
+                s_ps, d_ps = acc[a]
+                ts = slice(t * O, (t + 1) * O)
+                nc.scalar.activation(out=sc[:, ts], in_=s_ps[:], func=ACT.Copy, scale=SCALE)
+                tt = ttp.tile([P, O], F32, name="tt")
+                nc.vector.tensor_tensor(out=tt[:], in0=sc[:, ts], in1=gate_ps[:], op=ALU.subtract)
+                mm = mmp.tile([P, O], F32, name="mm")
+                nc.vector.scalar_tensor_tensor(
+                    out=mm[:], in0=tt[:], scalar=0.0, in1=d_ps[:], op0=ALU.max, op1=ALU.mult
+                )
+                nc.gpsimd.tensor_tensor(out=mk[:, ts], in0=mm[:], in1=bias_sb[:], op=ALU.add)
+                if i in FLUSH_AFTER:
+                    lo = outs["lo"]
+                    sc3 = sc[:].rearrange("p (t o) -> p t o", t=T)
+                    mk3 = mk[:].rearrange("p (t o) -> p t o", t=T)
+                    nc.sync.dma_start(out=ov1[c][:, lo : t + 1, :], in_=sc3[:, lo : t + 1, :])
+                    nc.sync.dma_start(out=ov0[c][:, lo : t + 1, :], in_=mk3[:, lo : t + 1, :])
+                    nc.sync.dma_start(out=ov2[c][:, lo : t + 1, :], in_=mk3[:, lo : t + 1, :])
+                    outs["lo"] = t + 1

@@ -21,8 +21,8 @@ NPAIR = ROWS // (2 * P)
 NJ = O // P
 SCALE = 1.0 / 32.0
 CLAMP = 32.0
-LOOKAHEAD = 2
-FLUSH_AFTER = (1, 3, 7, 11, 15, 19, 23, 27, 29, 30, 31)
+FLUSH_AFTER = (0, 1, 2, 3, 5, 7, 9, 11, 13, 14, 15)
+FINE = (0, NPAIR - 1)
 
 FLOPS = 2 * 2 * ROWS * K * O
 
@@ -37,15 +37,16 @@ def tile_sparsebayesianlinear_t_kernel(
     ov2 = out_2.rearrange("(c p t) o -> c p t o", c=NCH, p=P)
 
     with ExitStack() as ctx:
+        ctx.enter_context(tc.manual_schedule())
         const = ctx.enter_context(tc.tile_pool(name="const", bufs=1))
         wts = ctx.enter_context(tc.tile_pool(name="wts", bufs=1))
         xin = ctx.enter_context(tc.tile_pool(name="xin", bufs=1))
         xgp = ctx.enter_context(tc.tile_pool(name="xgp", bufs=3))
-        xcp = ctx.enter_context(tc.tile_pool(name="xcp", bufs=6))
+        xcp = ctx.enter_context(tc.tile_pool(name="xcp", bufs=4))
         scp = ctx.enter_context(tc.tile_pool(name="scp", bufs=3))
         mkp = ctx.enter_context(tc.tile_pool(name="mkp", bufs=3))
         ttp = ctx.enter_context(tc.tile_pool(name="ttp", bufs=2))
-        mmp = ctx.enter_context(tc.tile_pool(name="mmp", bufs=3))
+        mmp = ctx.enter_context(tc.tile_pool(name="mmp", bufs=2))
         psg = ctx.enter_context(tc.psum_pool(name="psg", bufs=1))
         psx = ctx.enter_context(tc.psum_pool(name="psx", bufs=2))
         pss = ctx.enter_context(tc.psum_pool(name="pss", bufs=2))
@@ -90,54 +91,108 @@ def tile_sparsebayesianlinear_t_kernel(
         vcl32 = vcl[:].bitcast(F32)
         sig32 = sig[:].bitcast(F32)
         mur32 = mur[:].bitcast(F32)
-        vc_pools = (pss, pss, psd, psd)
-        for j in range(NJ):
-            js = slice(j * K, (j + 1) * K)
-            nc.vector.tensor_scalar_min(out=vcl[:, js], in0=sig[:, js], scalar1=CLAMP)
-            bank = vc_pools[j].tile([P, O], F32, name="bk")
-            transpose_words(vcl32, j * (K // 2), bank)
-            nc.scalar.activation(out=elog[:, js], in_=bank[:].bitcast(BF16), func=ACT.Exp)
-
-        gate_ps = psg.tile([P, O], F32, name="gate_ps")
-        nc.tensor.matmul(out=gate_ps[:], lhsT=ones[:], rhs=vecs[:, 0:O], start=True, stop=True)
-        bias_ps = psx.tile([P, O], F32, name="bk")
-        nc.tensor.matmul(out=bias_ps[:], lhsT=ones[:], rhs=vecs[:, O : 2 * O], start=True, stop=True)
-
-        for j in range(NJ):
-            js = slice(j * K, (j + 1) * K)
-            nc.vector.tensor_scalar(
-                out=sig[:, js], in0=sig[:, js], scalar1=1.0 / CLAMP, scalar2=1.0, op0=ALU.mult, op1=ALU.max
-            )
-        nc.vector.tensor_copy(out=bias_sb[:], in_=bias_ps[:])
-        for j in range(NJ):
-            js = slice(j * K, (j + 1) * K)
-            nc.vector.tensor_tensor(out=sig[:, js], in0=sig[:, js], in1=mur[:, js], op=ALU.mult)
-
         mu_g32 = mu_g[:].bitcast(F32).rearrange("p (g o u) -> p g o u", g=2, u=2)
-        mu_pools = (psd, psx, psx, psx)
-        for j in range(NJ):
-            bank = mu_pools[j].tile([P, O], F32, name="bk")
-            transpose_words(mur32, j * (K // 2), bank)
+
+        def mu_copy(j, bank):
             nc.vector.tensor_copy(
                 out=mu_g32[:, :, j * P : (j + 1) * P, :],
                 in_=bank[:].rearrange("p (g u r) -> p g r u", g=2, u=2),
             )
+
+        xbanks = {}
+        xgs = {}
+        codes = {}
+
+        def x_transpose(q):
+            x32 = x_sb[q // 2][:].bitcast(F32)
+            banks = []
+            for a in range(2):
+                bank = psx.tile([P, O], F32, name="bk")
+                transpose_words(x32, ((q % 2) * 2 + a) * (K // 2), bank)
+                banks.append(bank)
+            xbanks[q] = banks
+
+        def x_copy(q):
+            xg = xgp.tile([P, 2 * K], BF16, name="xg", align_bytes=64)
+            xg32 = xg[:].bitcast(F32).rearrange("p (a g r u) -> p a g r u", a=2, g=2, u=2)
+            for a in range(2):
+                nc.scalar.copy(
+                    out=xg32[:, a], in_=xbanks[q][a][:].rearrange("p (g u r) -> p g r u", g=2, u=2)
+                )
+            xgs[q] = xg
+
+        def x_quant(q):
+            xc = xcp.tile([P, 2 * 2 * P], U32, name="xc", align_bytes=64)
+            xs = xcp.tile([P, 2 * 2 * P], U8, name="xs", align_bytes=64)
+            nc.vector.quantize_mx(out=xc[:].bitcast(FP8X4), scales=xs[:], in_=xgs[q][:])
+            codes[q] = (xc, xs)
+
+        def mx_pass(q, a, g, w, ps):
+            xc, xs = codes[q]
+            l0 = a * 2 * P + g * P
+            w0 = w * 2 * O + g * O
+            nc.tensor.matmul_mx(
+                out=ps[:],
+                lhsT=xc[:, l0 : l0 + P].bitcast(FP8X4),
+                lhsT_scale=xs[:, l0 : l0 + P],
+                rhs=wc[:, w0 : w0 + O].bitcast(FP8X4),
+                rhs_scale=ws[:, w0 : w0 + O],
+                start=(g == 0),
+                stop=(g == 1),
+            )
+
+        vc_pools = (pss, pss, psd, psd)
+        mu_banks = {}
+        for j in range(NJ):
+            js = slice(j * K, (j + 1) * K)
+            nc.vector.tensor_scalar_min(out=vcl[:, js], in0=sig[:, js], scalar1=CLAMP)
+            nc.vector.tensor_scalar(
+                out=sig[:, js], in0=sig[:, js], scalar1=1.0 / CLAMP, scalar2=1.0, op0=ALU.mult, op1=ALU.max
+            )
+            bank = vc_pools[j].tile([P, O], F32, name="bk")
+            transpose_words(vcl32, j * (K // 2), bank)
+            nc.scalar.activation(out=elog[:, js], in_=bank[:].bitcast(BF16), func=ACT.Exp)
+            mbank = psx.tile([P, O], F32, name="bk")
+            transpose_words(mur32, j * (K // 2), mbank)
+            mu_banks[j] = mbank
+            if j >= 1:
+                mu_copy(j - 1, mu_banks[j - 1])
+            if j < 2:
+                nc.gpsimd.tensor_tensor(out=sig[:, js], in0=sig[:, js], in1=mur[:, js], op=ALU.mult)
+        mu_copy(NJ - 1, mu_banks[NJ - 1])
+
+        gate_ps = psg.tile([P, O], F32, name="gate_ps")
+        nc.tensor.matmul(out=gate_ps[:], lhsT=ones[:], rhs=vecs[:, 0:O], start=True, stop=True)
+        bias_ps = psd.tile([P, O], F32, name="bk")
+        nc.tensor.matmul(out=bias_ps[:], lhsT=ones[:], rhs=vecs[:, O : 2 * O], start=True, stop=True)
+
         for g in range(2):
             nc.vector.quantize_mx(
                 out=wc[:, g * O : (g + 1) * O].bitcast(FP8X4),
                 scales=ws[:, g * O : (g + 1) * O],
                 in_=mu_g[:, g * 4 * O : (g + 1) * 4 * O],
             )
+        for j in range(2, NJ):
+            js = slice(j * K, (j + 1) * K)
+            nc.vector.tensor_tensor(out=sig[:, js], in0=sig[:, js], in1=mur[:, js], op=ALU.mult)
+
         m2_pools = (pss, pss, psd, psd)
         m2_banks = []
         for j in range(NJ):
+            if j == 2:
+                x_transpose(0)
             bank = m2_pools[j].tile([P, O], F32, name="bk")
             transpose_words(sig32, j * (K // 2), bank)
             m2_banks.append(bank)
 
         for j in range(NJ):
             js = slice(j * K, (j + 1) * K)
+            if j == NJ - 1:
+                x_copy(0)
+                x_transpose(1)
             nc.scalar.activation(out=elog[:, js], in_=elog[:, js], func=ACT.Ln, bias=1.0)
+            if j == NJ - 1:
+                x_quant(0)
             m2v = m2_banks[j][:].bitcast(BF16)
             for g in range(2):
                 nc.vector.tensor_tensor(
@@ -157,81 +212,74 @@ def tile_sparsebayesianlinear_t_kernel(
                     scales=ws[:, w0 : w0 + P],
                     in_=keys_g[:, g * 4 * O + j * 4 * P : g * 4 * O + (j + 1) * 4 * P],
                 )
+        nc.scalar.copy(out=bias_sb[:], in_=bias_ps[:])
+        x_copy(1)
+        x_quant(1)
 
-        def prep(q):
-            c = q // 2
-            t0 = (q % 2) * 2
-            x32 = x_sb[c][:].bitcast(F32)
-            xg = xgp.tile([P, 2 * K], BF16, name="xg", align_bytes=64)
-            xg32 = xg[:].bitcast(F32).rearrange("p (a g r u) -> p a g r u", a=2, g=2, u=2)
-            banks = []
-            for a in range(2):
-                bank = psx.tile([P, O], F32, name="bk")
-                transpose_words(x32, (t0 + a) * (K // 2), bank)
-                banks.append(bank)
-            for a in range(2):
-                nc.scalar.copy(
-                    out=xg32[:, a], in_=banks[a][:].rearrange("p (g u r) -> p g r u", g=2, u=2)
-                )
-            xc = xcp.tile([P, 2 * 2 * P], U32, name="xc", align_bytes=64)
-            xs = xcp.tile([P, 2 * 2 * P], U8, name="xs", align_bytes=64)
-            nc.vector.quantize_mx(out=xc[:].bitcast(FP8X4), scales=xs[:], in_=xg[:])
-            return xc, xs
-
-        codes = {}
-        for q in range(LOOKAHEAD):
-            codes[q] = prep(q)
-
+        bias_bc = bias_sb[:].unsqueeze(1).to_broadcast([P, 2, O])
         outs = {}
         for q in range(NPAIR):
-            if q + LOOKAHEAD < NPAIR:
-                codes[q + LOOKAHEAD] = prep(q + LOOKAHEAD)
-            xc, xs = codes[q]
-            acc = []
+            c = q // 2
+            t0 = (q % 2) * 2
+            if t0 == 0:
+                sc_new = scp.tile([P, T * O], F32, name="sc")
+                mk_new = mkp.tile([P, T * O], F32, name="mk")
+                outs["sc"] = sc_new
+                outs["mk"] = mk_new
+                outs["lo"] = 0
+            sc = outs["sc"]
+            mk = outs["mk"]
+            lo = outs["lo"]
+            hi = t0 + 2
+            sc3 = sc[:].rearrange("p (t o) -> p t o", t=T)
+            mk3 = mk[:].rearrange("p (t o) -> p t o", t=T)
+
+            d_ps = [psd.tile([P, O], F32, name="bk") for a in range(2)]
+            s_ps = [pss.tile([P, O], F32, name="bk") for a in range(2)]
+            if q == 0:
+                for a in range(2):
+                    for g in range(2):
+                        mx_pass(q, a, g, 0, d_ps[a])
+                for a in range(2):
+                    for g in range(2):
+                        mx_pass(q, a, g, 1, s_ps[a])
+            else:
+                for a in range(2):
+                    for g in range(2):
+                        mx_pass(q, a, g, 1, s_ps[a])
+                        mx_pass(q, a, g, 0, d_ps[a])
+            fine = q in FINE
             for a in range(2):
-                d_ps = psd.tile([P, O], F32, name="bk")
-                s_ps = pss.tile([P, O], F32, name="bk")
-                for g in range(2):
-                    l0 = a * 2 * P + g * P
-                    for w, ps in ((0, d_ps), (1, s_ps)):
-                        w0 = w * 2 * O + g * O
-                        nc.tensor.matmul_mx(
-                            out=ps[:],
-                            lhsT=xc[:, l0 : l0 + P].bitcast(FP8X4),
-                            lhsT_scale=xs[:, l0 : l0 + P],
-                            rhs=wc[:, w0 : w0 + O].bitcast(FP8X4),
-                            rhs_scale=ws[:, w0 : w0 + O],
-                            start=(g == 0),
-                            stop=(g == 1),
-                        )
-                acc.append((s_ps, d_ps))
+                ts = slice((t0 + a) * O, (t0 + a + 1) * O)
+                nc.scalar.activation(out=sc[:, ts], in_=s_ps[a][:], func=ACT.Copy, scale=SCALE)
+                if fine:
+                    nc.sync.dma_start(out=ov1[c][:, t0 + a : t0 + a + 1, :], in_=sc3[:, t0 + a : t0 + a + 1, :])
+            if q in FLUSH_AFTER and not fine:
+                nc.sync.dma_start(out=ov1[c][:, lo:hi, :], in_=sc3[:, lo:hi, :])
+            if q + 2 < NPAIR:
+                x_transpose(q + 2)
+                x_copy(q + 2)
+            mm = mmp.tile([P, 2 * O], F32, name="mm")
             for a in range(2):
-                i = 2 * q + a
-                c = i // T
-                t = i % T
-                if t == 0:
-                    sc_new = scp.tile([P, T * O], F32, name="sc")
-                    mk_new = mkp.tile([P, T * O], F32, name="mk")
-                    outs["sc"] = sc_new
-                    outs["mk"] = mk_new
-                    outs["lo"] = 0
-                sc = outs["sc"]
-                mk = outs["mk"]
-                s_ps, d_ps = acc[a]
-                ts = slice(t * O, (t + 1) * O)
-                nc.scalar.activation(out=sc[:, ts], in_=s_ps[:], func=ACT.Copy, scale=SCALE)
+                ts = slice((t0 + a) * O, (t0 + a + 1) * O)
                 tt = ttp.tile([P, O], F32, name="tt")
                 nc.vector.tensor_tensor(out=tt[:], in0=sc[:, ts], in1=gate_ps[:], op=ALU.subtract)
-                mm = mmp.tile([P, O], F32, name="mm")
                 nc.vector.scalar_tensor_tensor(
-                    out=mm[:], in0=tt[:], scalar=0.0, in1=d_ps[:], op0=ALU.max, op1=ALU.mult
+                    out=mm[:, a * O : (a + 1) * O], in0=tt[:], scalar=0.0, in1=d_ps[a][:], op0=ALU.max, op1=ALU.mult
                 )
-                nc.gpsimd.tensor_tensor(out=mk[:, ts], in0=mm[:], in1=bias_sb[:], op=ALU.add)
-                if i in FLUSH_AFTER:
-                    lo = outs["lo"]
-                    sc3 = sc[:].rearrange("p (t o) -> p t o", t=T)
-                    mk3 = mk[:].rearrange("p (t o) -> p t o", t=T)
-                    nc.sync.dma_start(out=ov1[c][:, lo : t + 1, :], in_=sc3[:, lo : t + 1, :])
-                    nc.sync.dma_start(out=ov0[c][:, lo : t + 1, :], in_=mk3[:, lo : t + 1, :])
-                    nc.sync.dma_start(out=ov2[c][:, lo : t + 1, :], in_=mk3[:, lo : t + 1, :])
-                    outs["lo"] = t + 1
+                if fine:
+                    adder = nc.vector if (q == NPAIR - 1 and a == 1) else nc.gpsimd
+                    adder.tensor_tensor(out=mk[:, ts], in0=mm[:, a * O : (a + 1) * O], in1=bias_sb[:], op=ALU.add)
+                    nc.sync.dma_start(out=ov0[c][:, t0 + a : t0 + a + 1, :], in_=mk3[:, t0 + a : t0 + a + 1, :])
+                    nc.sync.dma_start(out=ov2[c][:, t0 + a : t0 + a + 1, :], in_=mk3[:, t0 + a : t0 + a + 1, :])
+            if q + 2 < NPAIR:
+                x_quant(q + 2)
+            if not fine:
+                nc.gpsimd.tensor_tensor(
+                    out=mk3[:, t0:hi, :], in0=mm[:].rearrange("p (a o) -> p a o", a=2), in1=bias_bc, op=ALU.add
+                )
+            if q in FLUSH_AFTER:
+                if not fine:
+                    nc.sync.dma_start(out=ov0[c][:, lo:hi, :], in_=mk3[:, lo:hi, :])
+                    nc.sync.dma_start(out=ov2[c][:, lo:hi, :], in_=mk3[:, lo:hi, :])
+                outs["lo"] = hi

@@ -21,8 +21,8 @@ NPAIR = ROWS // (2 * P)
 NJ = O // P
 SCALE = 1.0 / 32.0
 CLAMP = 32.0
-FLUSH_AFTER = (0, 1, 2, 3, 5, 7, 9, 11, 13, 14, 15)
-FINE = (0, NPAIR - 1)
+FLUSH_AFTER = (0,1,2,3,4,5,7,9,11,13,14,15)
+FINE = (NPAIR - 1,)
 
 FLOPS = 2 * 2 * ROWS * K * O
 
@@ -157,8 +157,6 @@ def tile_sparsebayesianlinear_t_kernel(
             mu_banks[j] = mbank
             if j >= 1:
                 mu_copy(j - 1, mu_banks[j - 1])
-            if j < 2:
-                nc.gpsimd.tensor_tensor(out=sig[:, js], in0=sig[:, js], in1=mur[:, js], op=ALU.mult)
         mu_copy(NJ - 1, mu_banks[NJ - 1])
 
         gate_ps = psg.tile([P, O], F32, name="gate_ps")
@@ -166,15 +164,15 @@ def tile_sparsebayesianlinear_t_kernel(
         bias_ps = psd.tile([P, O], F32, name="bk")
         nc.tensor.matmul(out=bias_ps[:], lhsT=ones[:], rhs=vecs[:, O : 2 * O], start=True, stop=True)
 
+        for j in range(NJ):
+            js = slice(j * K, (j + 1) * K)
+            nc.vector.tensor_tensor(out=sig[:, js], in0=sig[:, js], in1=mur[:, js], op=ALU.mult)
         for g in range(2):
             nc.vector.quantize_mx(
                 out=wc[:, g * O : (g + 1) * O].bitcast(FP8X4),
                 scales=ws[:, g * O : (g + 1) * O],
                 in_=mu_g[:, g * 4 * O : (g + 1) * 4 * O],
             )
-        for j in range(2, NJ):
-            js = slice(j * K, (j + 1) * K)
-            nc.vector.tensor_tensor(out=sig[:, js], in0=sig[:, js], in1=mur[:, js], op=ALU.mult)
 
         m2_pools = (pss, pss, psd, psd)
         m2_banks = []
@@ -260,12 +258,16 @@ def tile_sparsebayesianlinear_t_kernel(
                 x_transpose(q + 2)
                 x_copy(q + 2)
             mm = mmp.tile([P, 2 * O], F32, name="mm")
+            tts = []
             for a in range(2):
                 ts = slice((t0 + a) * O, (t0 + a + 1) * O)
                 tt = ttp.tile([P, O], F32, name="tt")
                 nc.vector.tensor_tensor(out=tt[:], in0=sc[:, ts], in1=gate_ps[:], op=ALU.subtract)
+                tts.append(tt)
+            for a in range(2):
+                ts = slice((t0 + a) * O, (t0 + a + 1) * O)
                 nc.vector.scalar_tensor_tensor(
-                    out=mm[:, a * O : (a + 1) * O], in0=tt[:], scalar=0.0, in1=d_ps[a][:], op0=ALU.max, op1=ALU.mult
+                    out=mm[:, a * O : (a + 1) * O], in0=tts[a][:], scalar=0.0, in1=d_ps[a][:], op0=ALU.max, op1=ALU.mult
                 )
                 if fine:
                     adder = nc.vector if (q == NPAIR - 1 and a == 1) else nc.gpsimd

@@ -22,7 +22,7 @@ NJ = O // P
 SCALE = 1.0 / 32.0
 CLAMP = 32.0
 FLUSH_AFTER = (0,1,2,3,4,5,7,9,11,13,14,15)
-FINE = (NPAIR - 1,)
+FINE = ()
 
 FLOPS = 2 * 2 * ROWS * K * O
 
@@ -167,12 +167,6 @@ def tile_sparsebayesianlinear_t_kernel(
         for j in range(NJ):
             js = slice(j * K, (j + 1) * K)
             nc.vector.tensor_tensor(out=sig[:, js], in0=sig[:, js], in1=mur[:, js], op=ALU.mult)
-        for g in range(2):
-            nc.vector.quantize_mx(
-                out=wc[:, g * O : (g + 1) * O].bitcast(FP8X4),
-                scales=ws[:, g * O : (g + 1) * O],
-                in_=mu_g[:, g * 4 * O : (g + 1) * 4 * O],
-            )
 
         m2_pools = (pss, pss, psd, psd)
         m2_banks = []
@@ -188,7 +182,9 @@ def tile_sparsebayesianlinear_t_kernel(
             if j == NJ - 1:
                 x_copy(0)
                 x_transpose(1)
-            nc.scalar.activation(out=elog[:, js], in_=elog[:, js], func=ACT.Ln, bias=1.0)
+            for g in range(2):
+                gs = slice(j * K + g * 512, j * K + (g + 1) * 512)
+                nc.scalar.activation(out=elog[:, gs], in_=elog[:, gs], func=ACT.Ln, bias=1.0)
             if j == NJ - 1:
                 x_quant(0)
             m2v = m2_banks[j][:].bitcast(BF16)
@@ -210,12 +206,27 @@ def tile_sparsebayesianlinear_t_kernel(
                     scales=ws[:, w0 : w0 + P],
                     in_=keys_g[:, g * 4 * O + j * 4 * P : g * 4 * O + (j + 1) * 4 * P],
                 )
+        for g in range(2):
+            nc.vector.quantize_mx(
+                out=wc[:, g * O : (g + 1) * O].bitcast(FP8X4),
+                scales=ws[:, g * O : (g + 1) * O],
+                in_=mu_g[:, g * 4 * O : (g + 1) * 4 * O],
+            )
         nc.scalar.copy(out=bias_sb[:], in_=bias_ps[:])
         x_copy(1)
         x_quant(1)
+        x_transpose(2)
+        x_copy(2)
 
         bias_bc = bias_sb[:].unsqueeze(1).to_broadcast([P, 2, O])
         outs = {}
+        outs["pend"] = []
+
+        def emit_pending():
+            for dst, src_ap in outs["pend"]:
+                nc.sync.dma_start(out=dst, in_=src_ap)
+            outs["pend"] = []
+
         for q in range(NPAIR):
             c = q // 2
             t0 = (q % 2) * 2
@@ -237,10 +248,10 @@ def tile_sparsebayesianlinear_t_kernel(
             if q == 0:
                 for a in range(2):
                     for g in range(2):
-                        mx_pass(q, a, g, 0, d_ps[a])
+                        mx_pass(q, a, g, 1, s_ps[a])
                 for a in range(2):
                     for g in range(2):
-                        mx_pass(q, a, g, 1, s_ps[a])
+                        mx_pass(q, a, g, 0, d_ps[a])
             else:
                 for a in range(2):
                     for g in range(2):
@@ -254,9 +265,10 @@ def tile_sparsebayesianlinear_t_kernel(
                     nc.sync.dma_start(out=ov1[c][:, t0 + a : t0 + a + 1, :], in_=sc3[:, t0 + a : t0 + a + 1, :])
             if q in FLUSH_AFTER and not fine:
                 nc.sync.dma_start(out=ov1[c][:, lo:hi, :], in_=sc3[:, lo:hi, :])
-            if q + 2 < NPAIR:
-                x_transpose(q + 2)
-                x_copy(q + 2)
+            emit_pending()
+            if q + 3 < NPAIR:
+                x_transpose(q + 3)
+                x_copy(q + 3)
             mm = mmp.tile([P, 2 * O], F32, name="mm")
             tts = []
             for a in range(2):
@@ -282,6 +294,7 @@ def tile_sparsebayesianlinear_t_kernel(
                 )
             if q in FLUSH_AFTER:
                 if not fine:
-                    nc.sync.dma_start(out=ov0[c][:, lo:hi, :], in_=mk3[:, lo:hi, :])
-                    nc.sync.dma_start(out=ov2[c][:, lo:hi, :], in_=mk3[:, lo:hi, :])
+                    outs["pend"].append((ov0[c][:, lo:hi, :], mk3[:, lo:hi, :]))
+                    outs["pend"].append((ov2[c][:, lo:hi, :], mk3[:, lo:hi, :]))
                 outs["lo"] = hi
+        emit_pending()

@@ -22,7 +22,7 @@ NJ = O // P
 SCALE = 1.0 / 32.0
 CLAMP = 32.0
 FLUSH_AFTER = (0,1,2,3,4,5,7,9,11,13,14,15)
-FINE = ()
+FINE = (NPAIR - 1,)
 
 FLOPS = 2 * 2 * ROWS * K * O
 

@@ -21,7 +21,7 @@ NPAIR = ROWS // (2 * P)
 NJ = O // P
 SCALE = 1.0 / 32.0
 CLAMP = 32.0
-FLUSH_AFTER = (0,1,2,3,4,5,7,9,11,13,14,15)
+FLUSH_AFTER = tuple(range(16))
 FINE = (NPAIR - 1,)
 
 FLOPS = 2 * 2 * ROWS * K * O

@@ -57,7 +57,9 @@ def tile_sparsebayesianlinear_t_kernel(
         ones = const.tile([P, P], BF16, name="ones")
         nc.vector.memset(ones[:], 1.0)
         vecs = const.tile([P, 2 * O], BF16, name="vecs")
-        nc.vector.memset(vecs[:], 0.0)
+        nc.vector.memset(vecs[:].bitcast(U32), 0)
+        warm = const.tile([P, 1], F32, name="warm")
+        nc.scalar.activation(out=warm[:], in_=ones[:, 0:1], func=ACT.Exp)
         nc.scalar.dma_start(out=vecs[0:1, 0:O], in_=gate_param.unsqueeze(0))
         nc.scalar.dma_start(out=vecs[0:1, O : 2 * O], in_=mu_bias.unsqueeze(0))
         bias_sb = const.tile([P, O], F32, name="bias_sb")
@@ -73,6 +75,7 @@ def tile_sparsebayesianlinear_t_kernel(
 
         for j in range(NJ):
             nc.sync.dma_start(out=sig[:, j * K : (j + 1) * K], in_=sigma_weight[j * P : (j + 1) * P, :])
+        for j in range(NJ):
             nc.sync.dma_start(out=mur[:, j * K : (j + 1) * K], in_=mu_weight[j * P : (j + 1) * P, :])
         x_sb = []
         for c in range(NCH):
@@ -103,13 +106,15 @@ def tile_sparsebayesianlinear_t_kernel(
         xgs = {}
         codes = {}
 
-        def x_transpose(q):
+        def x_transpose(q, warm=0):
             x32 = x_sb[q // 2][:].bitcast(F32)
             banks = []
             for a in range(2):
                 bank = psx.tile([P, O], F32, name="bk")
                 transpose_words(x32, ((q % 2) * 2 + a) * (K // 2), bank)
                 banks.append(bank)
+                if warm:
+                    warm_up(warm)
             xbanks[q] = banks
 
         def x_copy(q):
@@ -141,52 +146,79 @@ def tile_sparsebayesianlinear_t_kernel(
                 stop=(g == 1),
             )
 
-        vc_pools = (pss, pss, psd, psd)
-        mu_banks = {}
-        for j in range(NJ):
+        w_pools = (pss, pss, psd, psd)
+
+        def softplus_exp(j):
             js = slice(j * K, (j + 1) * K)
             nc.vector.tensor_scalar_min(out=vcl[:, js], in0=sig[:, js], scalar1=CLAMP)
+            bank = w_pools[j].tile([P, O], F32, name="bk")
+            transpose_words(vcl32, j * (K // 2), bank)
+            nc.scalar.activation(out=elog[:, js], in_=bank[:].bitcast(BF16), func=ACT.Exp)
+
+        def excess(j):
+            js = slice(j * K, (j + 1) * K)
             nc.vector.tensor_scalar(
                 out=sig[:, js], in0=sig[:, js], scalar1=1.0 / CLAMP, scalar2=1.0, op0=ALU.mult, op1=ALU.max
             )
-            bank = vc_pools[j].tile([P, O], F32, name="bk")
-            transpose_words(vcl32, j * (K // 2), bank)
-            nc.scalar.activation(out=elog[:, js], in_=bank[:].bitcast(BF16), func=ACT.Exp)
-            mbank = psx.tile([P, O], F32, name="bk")
-            transpose_words(mur32, j * (K // 2), mbank)
-            mu_banks[j] = mbank
-            if j >= 1:
-                mu_copy(j - 1, mu_banks[j - 1])
-        mu_copy(NJ - 1, mu_banks[NJ - 1])
+
+        mu_banks = {}
+        m2_banks = {}
+
+        def mu_transpose(j):
+            bank = psx.tile([P, O], F32, name="bk")
+            transpose_words(mur32, j * (K // 2), bank)
+            mu_banks[j] = bank
+
+        def m2_make(j):
+            js = slice(j * K, (j + 1) * K)
+            nc.vector.tensor_tensor(out=sig[:, js], in0=sig[:, js], in1=mur[:, js], op=ALU.mult)
+            bank = w_pools[j].tile([P, O], F32, name="bk")
+            transpose_words(sig32, j * (K // 2), bank)
+            m2_banks[j] = bank
+
+        softplus_exp(0)
+        softplus_exp(1)
+        excess(0)
+        softplus_exp(2)
+        excess(1)
+        softplus_exp(3)
+        excess(2)
+        excess(3)
+        mu_transpose(0)
+        mu_transpose(1)
+        m2_make(0)
+        m2_make(1)
+        mu_copy(0, mu_banks[0])
+        mu_transpose(2)
+        m2_make(2)
+        mu_copy(1, mu_banks[1])
+        mu_transpose(3)
+        m2_make(3)
+        mu_copy(2, mu_banks[2])
+        mu_copy(3, mu_banks[3])
+        x_transpose(0)
 
         gate_ps = psg.tile([P, O], F32, name="gate_ps")
-        nc.tensor.matmul(out=gate_ps[:], lhsT=ones[:], rhs=vecs[:, 0:O], start=True, stop=True)
+
+        def warm_up(n):
+            for i in range(n):
+                nc.tensor.matmul(out=gate_ps[:], lhsT=ones[:], rhs=keys_g[:, 4 * P : 2 * 4 * P], start=True, stop=True)
+
         bias_ps = psd.tile([P, O], F32, name="bk")
         nc.tensor.matmul(out=bias_ps[:], lhsT=ones[:], rhs=vecs[:, O : 2 * O], start=True, stop=True)
 
+        for g in range(2):
+            nc.vector.quantize_mx(
+                out=wc[:, g * O : (g + 1) * O].bitcast(FP8X4),
+                scales=ws[:, g * O : (g + 1) * O],
+                in_=mu_g[:, g * 4 * O : (g + 1) * 4 * O],
+            )
         for j in range(NJ):
-            js = slice(j * K, (j + 1) * K)
-            nc.vector.tensor_tensor(out=sig[:, js], in0=sig[:, js], in1=mur[:, js], op=ALU.mult)
-
-        m2_pools = (pss, pss, psd, psd)
-        m2_banks = []
-        for j in range(NJ):
-            if j == 2:
-                x_transpose(0)
-            bank = m2_pools[j].tile([P, O], F32, name="bk")
-            transpose_words(sig32, j * (K // 2), bank)
-            m2_banks.append(bank)
-
-        for j in range(NJ):
-            js = slice(j * K, (j + 1) * K)
-            if j == NJ - 1:
-                x_copy(0)
-                x_transpose(1)
             for g in range(2):
                 gs = slice(j * K + g * 512, j * K + (g + 1) * 512)
                 nc.scalar.activation(out=elog[:, gs], in_=elog[:, gs], func=ACT.Ln, bias=1.0)
             if j == NJ - 1:
-                x_quant(0)
+                warm_up(4)
             m2v = m2_banks[j][:].bitcast(BF16)
             for g in range(2):
                 nc.vector.tensor_tensor(
@@ -199,6 +231,10 @@ def tile_sparsebayesianlinear_t_kernel(
                     in1=m2v[:, g * 512 : (g + 1) * 512].rearrange("p (u r e) -> p r u e", u=2, e=2),
                     op=ALU.mult,
                 )
+            if j == NJ - 1:
+                x_copy(0)
+                x_transpose(1, 1)
+                x_quant(0)
             for g in range(2):
                 w0 = 2 * O + g * O + j * P
                 nc.vector.quantize_mx(
@@ -206,17 +242,12 @@ def tile_sparsebayesianlinear_t_kernel(
                     scales=ws[:, w0 : w0 + P],
                     in_=keys_g[:, g * 4 * O + j * 4 * P : g * 4 * O + (j + 1) * 4 * P],
                 )
-        for g in range(2):
-            nc.vector.quantize_mx(
-                out=wc[:, g * O : (g + 1) * O].bitcast(FP8X4),
-                scales=ws[:, g * O : (g + 1) * O],
-                in_=mu_g[:, g * 4 * O : (g + 1) * 4 * O],
-            )
-        nc.scalar.copy(out=bias_sb[:], in_=bias_ps[:])
         x_copy(1)
         x_quant(1)
-        x_transpose(2)
+        x_transpose(2, 1)
+        nc.tensor.matmul(out=gate_ps[:], lhsT=ones[:], rhs=vecs[:, 0:O], start=True, stop=True)
         x_copy(2)
+        nc.scalar.copy(out=bias_sb[:], in_=bias_ps[:])
 
         bias_bc = bias_sb[:].unsqueeze(1).to_broadcast([P, 2, O])
         outs = {}
@@ -246,12 +277,10 @@ def tile_sparsebayesianlinear_t_kernel(
             d_ps = [psd.tile([P, O], F32, name="bk") for a in range(2)]
             s_ps = [pss.tile([P, O], F32, name="bk") for a in range(2)]
             if q == 0:
-                for a in range(2):
-                    for g in range(2):
-                        mx_pass(q, a, g, 1, s_ps[a])
-                for a in range(2):
-                    for g in range(2):
-                        mx_pass(q, a, g, 0, d_ps[a])
+                for w, ps in ((1, s_ps), (0, d_ps)):
+                    for a in range(2):
+                        for g in range(2):
+                            mx_pass(q, a, g, w, ps[a])
             else:
                 for a in range(2):
                     for g in range(2):
@@ -266,9 +295,9 @@ def tile_sparsebayesianlinear_t_kernel(
             if q in FLUSH_AFTER and not fine:
                 nc.sync.dma_start(out=ov1[c][:, lo:hi, :], in_=sc3[:, lo:hi, :])
             emit_pending()
-            if q + 3 < NPAIR:
-                x_transpose(q + 3)
-                x_copy(q + 3)
+            if 1 <= q < NPAIR - 2:
+                x_transpose(q + 2)
+                x_copy(q + 2)
             mm = mmp.tile([P, 2 * O], F32, name="mm")
             tts = []
             for a in range(2):

@@ -47,10 +47,9 @@ def tile_sparsebayesianlinear_t_kernel(
         mkp = ctx.enter_context(tc.tile_pool(name="mkp", bufs=3))
         ttp = ctx.enter_context(tc.tile_pool(name="ttp", bufs=2))
         mmp = ctx.enter_context(tc.tile_pool(name="mmp", bufs=2))
-        psg = ctx.enter_context(tc.psum_pool(name="psg", bufs=1))
         psx = ctx.enter_context(tc.psum_pool(name="psx", bufs=2))
         pss = ctx.enter_context(tc.psum_pool(name="pss", bufs=2))
-        psd = ctx.enter_context(tc.psum_pool(name="psd", bufs=3))
+        psd = ctx.enter_context(tc.psum_pool(name="psd", bufs=4))
 
         ident = const.tile([P, P], F32, name="ident")
         make_identity(nc, ident[:])
@@ -63,6 +62,7 @@ def tile_sparsebayesianlinear_t_kernel(
         nc.scalar.dma_start(out=vecs[0:1, 0:O], in_=gate_param.unsqueeze(0))
         nc.scalar.dma_start(out=vecs[0:1, O : 2 * O], in_=mu_bias.unsqueeze(0))
         bias_sb = const.tile([P, O], F32, name="bias_sb")
+        gate_sb = const.tile([P, O], F32, name="gate_sb")
 
         sig = wts.tile([P, NJ * K], BF16, name="sig")
         mur = wts.tile([P, NJ * K], BF16, name="mur")
@@ -198,14 +198,13 @@ def tile_sparsebayesianlinear_t_kernel(
         mu_copy(3, mu_banks[3])
         x_transpose(0)
 
-        gate_ps = psg.tile([P, O], F32, name="gate_ps")
+        warm_ps = psd.tile([P, O], F32, name="bk")
+        bias_ps = psd.tile([P, O], F32, name="bk")
+        nc.tensor.matmul(out=bias_ps[:], lhsT=ones[:], rhs=vecs[:, O : 2 * O], start=True, stop=True)
 
         def warm_up(n):
             for i in range(n):
-                nc.tensor.matmul(out=gate_ps[:], lhsT=ones[:], rhs=keys_g[:, 4 * P : 2 * 4 * P], start=True, stop=True)
-
-        bias_ps = psd.tile([P, O], F32, name="bk")
-        nc.tensor.matmul(out=bias_ps[:], lhsT=ones[:], rhs=vecs[:, O : 2 * O], start=True, stop=True)
+                nc.tensor.matmul(out=warm_ps[:], lhsT=ones[:], rhs=keys_g[:, 4 * P : 2 * 4 * P], start=True, stop=True)
 
         for g in range(2):
             nc.vector.quantize_mx(
@@ -244,10 +243,13 @@ def tile_sparsebayesianlinear_t_kernel(
                 )
         x_copy(1)
         x_quant(1)
-        x_transpose(2, 1)
+        gate_ps = psd.tile([P, O], F32, name="bk")
         nc.tensor.matmul(out=gate_ps[:], lhsT=ones[:], rhs=vecs[:, 0:O], start=True, stop=True)
+        x_transpose(2, 1)
         x_copy(2)
         nc.scalar.copy(out=bias_sb[:], in_=bias_ps[:])
+        nc.vector.tensor_copy(out=gate_sb[:], in_=gate_ps[:])
+        x_quant(2)
 
         bias_bc = bias_sb[:].unsqueeze(1).to_broadcast([P, 2, O])
         outs = {}
@@ -303,7 +305,9 @@ def tile_sparsebayesianlinear_t_kernel(
             for a in range(2):
                 ts = slice((t0 + a) * O, (t0 + a + 1) * O)
                 tt = ttp.tile([P, O], F32, name="tt")
-                nc.vector.tensor_tensor(out=tt[:], in0=sc[:, ts], in1=gate_ps[:], op=ALU.subtract)
+                nc.vector.scalar_tensor_tensor(
+                    out=tt[:], in0=s_ps[a][:], scalar=SCALE, in1=gate_sb[:], op0=ALU.mult, op1=ALU.subtract
+                )
                 tts.append(tt)
             for a in range(2):
                 ts = slice((t0 + a) * O, (t0 + a + 1) * O)
@@ -315,7 +319,7 @@ def tile_sparsebayesianlinear_t_kernel(
                     adder.tensor_tensor(out=mk[:, ts], in0=mm[:, a * O : (a + 1) * O], in1=bias_sb[:], op=ALU.add)
                     nc.sync.dma_start(out=ov0[c][:, t0 + a : t0 + a + 1, :], in_=mk3[:, t0 + a : t0 + a + 1, :])
                     nc.sync.dma_start(out=ov2[c][:, t0 + a : t0 + a + 1, :], in_=mk3[:, t0 + a : t0 + a + 1, :])
-            if q + 2 < NPAIR:
+            if 1 <= q < NPAIR - 2:
                 x_quant(q + 2)
             if not fine:
                 nc.gpsimd.tensor_tensor(

@@ -73,7 +73,10 @@ def tile_sparsebayesianlinear_t_kernel(
         wc = wts.tile([P, 2 * 2 * O], U32, name="wc", align_bytes=64)
         ws = wts.tile([P, 2 * 2 * O], U8, name="ws", align_bytes=64)
 
-        for j in range(NJ):
+        for half in range(2):
+            hs = slice(half * (K // 2), (half + 1) * (K // 2))
+            nc.sync.dma_start(out=sig[:, hs], in_=sigma_weight[0:P, hs])
+        for j in range(1, NJ):
             nc.sync.dma_start(out=sig[:, j * K : (j + 1) * K], in_=sigma_weight[j * P : (j + 1) * P, :])
         for j in range(NJ):
             nc.sync.dma_start(out=mur[:, j * K : (j + 1) * K], in_=mu_weight[j * P : (j + 1) * P, :])
@@ -146,14 +149,14 @@ def tile_sparsebayesianlinear_t_kernel(
                 stop=(g == 1),
             )
 
-        w_pools = (pss, pss, psd, psd)
-
-        def softplus_exp(j):
-            js = slice(j * K, (j + 1) * K)
-            nc.vector.tensor_scalar_min(out=vcl[:, js], in0=sig[:, js], scalar1=CLAMP)
-            bank = w_pools[j].tile([P, O], F32, name="bk")
-            transpose_words(vcl32, j * (K // 2), bank)
-            nc.scalar.activation(out=elog[:, js], in_=bank[:].bitcast(BF16), func=ACT.Exp)
+        def softplus_exp(j, bank, part, parts):
+            width = K // parts
+            cs = slice(j * K + part * width, j * K + (part + 1) * width)
+            nc.vector.tensor_scalar_min(out=vcl[:, cs], in0=sig[:, cs], scalar1=CLAMP)
+            for b in range(width // (2 * P)):
+                w = cs.start // 2 + b * P
+                nc.tensor.transpose(out=bank[:, b * P : (b + 1) * P], in_=vcl32[:, w : w + P], identity=ident[:])
+            nc.scalar.activation(out=elog[:, cs], in_=bank[:].bitcast(BF16)[:, 0:width], func=ACT.Exp)
 
         def excess(j):
             js = slice(j * K, (j + 1) * K)
@@ -169,55 +172,13 @@ def tile_sparsebayesianlinear_t_kernel(
             transpose_words(mur32, j * (K // 2), bank)
             mu_banks[j] = bank
 
-        def m2_make(j):
+        def m2_make(j, bank):
             js = slice(j * K, (j + 1) * K)
             nc.vector.tensor_tensor(out=sig[:, js], in0=sig[:, js], in1=mur[:, js], op=ALU.mult)
-            bank = w_pools[j].tile([P, O], F32, name="bk")
             transpose_words(sig32, j * (K // 2), bank)
             m2_banks[j] = bank
 
-        softplus_exp(0)
-        softplus_exp(1)
-        excess(0)
-        softplus_exp(2)
-        excess(1)
-        softplus_exp(3)
-        excess(2)
-        excess(3)
-        mu_transpose(0)
-        mu_transpose(1)
-        m2_make(0)
-        m2_make(1)
-        mu_copy(0, mu_banks[0])
-        mu_transpose(2)
-        m2_make(2)
-        mu_copy(1, mu_banks[1])
-        mu_transpose(3)
-        m2_make(3)
-        mu_copy(2, mu_banks[2])
-        mu_copy(3, mu_banks[3])
-        x_transpose(0)
-
-        warm_ps = psd.tile([P, O], F32, name="bk")
-        bias_ps = psd.tile([P, O], F32, name="bk")
-        nc.tensor.matmul(out=bias_ps[:], lhsT=ones[:], rhs=vecs[:, O : 2 * O], start=True, stop=True)
-
-        def warm_up(n):
-            for i in range(n):
-                nc.tensor.matmul(out=warm_ps[:], lhsT=ones[:], rhs=keys_g[:, 4 * P : 2 * 4 * P], start=True, stop=True)
-
-        for g in range(2):
-            nc.vector.quantize_mx(
-                out=wc[:, g * O : (g + 1) * O].bitcast(FP8X4),
-                scales=ws[:, g * O : (g + 1) * O],
-                in_=mu_g[:, g * 4 * O : (g + 1) * 4 * O],
-            )
-        for j in range(NJ):
-            for g in range(2):
-                gs = slice(j * K + g * 512, j * K + (g + 1) * 512)
-                nc.scalar.activation(out=elog[:, gs], in_=elog[:, gs], func=ACT.Ln, bias=1.0)
-            if j == NJ - 1:
-                warm_up(4)
+        def keys_mult(j):
             m2v = m2_banks[j][:].bitcast(BF16)
             for g in range(2):
                 nc.vector.tensor_tensor(
@@ -230,10 +191,8 @@ def tile_sparsebayesianlinear_t_kernel(
                     in1=m2v[:, g * 512 : (g + 1) * 512].rearrange("p (u r e) -> p r u e", u=2, e=2),
                     op=ALU.mult,
                 )
-            if j == NJ - 1:
-                x_copy(0)
-                x_transpose(1, 1)
-                x_quant(0)
+
+        def keys_quant(j):
             for g in range(2):
                 w0 = 2 * O + g * O + j * P
                 nc.vector.quantize_mx(
@@ -241,15 +200,89 @@ def tile_sparsebayesianlinear_t_kernel(
                     scales=ws[:, w0 : w0 + P],
                     in_=keys_g[:, g * 4 * O + j * 4 * P : g * 4 * O + (j + 1) * 4 * P],
                 )
-        x_copy(1)
-        x_quant(1)
+
+        def log_part(j, g):
+            gs = slice(j * K + g * 512, j * K + (g + 1) * 512)
+            nc.scalar.activation(out=elog[:, gs], in_=elog[:, gs], func=ACT.Ln, bias=1.0)
+
+        v_pools = (pss, pss, psd, psd)
+        v_half = psx.tile([P, O], F32, name="bk")
+        v_banks = [v_pools[j].tile([P, O], F32, name="bk") for j in range(NJ)]
+        softplus_exp(0, v_half, 0, 2)
+        softplus_exp(0, v_banks[0], 1, 2)
+        softplus_exp(1, v_banks[1], 0, 1)
+        excess(0)
+        softplus_exp(2, v_banks[2], 0, 1)
+        excess(1)
+        softplus_exp(3, v_banks[3], 0, 1)
+        excess(2)
+        excess(3)
+        mu_transpose(0)
+        mu_transpose(1)
+        warm_ps = psd.tile([P, O], F32, name="bk")
+        m2_pools = (pss, pss, psd, psd)
+        for j in range(NJ):
+            bank = m2_pools[j].tile([P, O], F32, name="bk")
+            m2_make(j, bank)
+            if j >= 2:
+                mu_copy(j - 2, mu_banks[j - 2])
+                mu_transpose(j)
+        mu_copy(2, mu_banks[2])
+        mu_copy(3, mu_banks[3])
         gate_ps = psd.tile([P, O], F32, name="bk")
         nc.tensor.matmul(out=gate_ps[:], lhsT=ones[:], rhs=vecs[:, 0:O], start=True, stop=True)
-        x_transpose(2, 1)
-        x_copy(2)
-        nc.scalar.copy(out=bias_sb[:], in_=bias_ps[:])
-        nc.vector.tensor_copy(out=gate_sb[:], in_=gate_ps[:])
-        x_quant(2)
+        x_transpose(0)
+
+        def warm_up(n):
+            for i in range(n):
+                nc.tensor.matmul(out=warm_ps[:], lhsT=ones[:], rhs=keys_g[:, 4 * P : 2 * 4 * P], start=True, stop=True)
+
+        def first_scores(j):
+            xc, xs = codes[0]
+            for a in range(2):
+                for g in range(2):
+                    l0 = a * 2 * P + g * P
+                    w0 = 2 * O + g * O + j * P
+                    nc.tensor.matmul_mx(
+                        out=s_first[a][:, j * P : (j + 1) * P],
+                        lhsT=xc[:, l0 : l0 + P].bitcast(FP8X4),
+                        lhsT_scale=xs[:, l0 : l0 + P],
+                        rhs=wc[:, w0 : w0 + P].bitcast(FP8X4),
+                        rhs_scale=ws[:, w0 : w0 + P],
+                        start=(g == 0),
+                        stop=(g == 1),
+                    )
+
+        for j in range(NJ - 1):
+            log_part(j, 0)
+            log_part(j, 1)
+            keys_mult(j)
+            keys_quant(j)
+        x_copy(0)
+        log_part(NJ - 1, 0)
+        log_part(NJ - 1, 1)
+        x_quant(0)
+        warm_up(2)
+        x_transpose(1, 1)
+        bias_ps = psd.tile([P, O], F32, name="bk")
+        nc.tensor.matmul(out=bias_ps[:], lhsT=ones[:], rhs=vecs[:, O : 2 * O], start=True, stop=True)
+        d_first = [psd.tile([P, O], F32, name="bk") for a in range(2)]
+        s_first = [pss.tile([P, O], F32, name="bk") for a in range(2)]
+        keys_mult(NJ - 1)
+        for j in range(NJ - 1):
+            first_scores(j)
+        keys_quant(NJ - 1)
+        first_scores(NJ - 1)
+        x_copy(1)
+        x_transpose(2)
+        nc.scalar.copy(out=gate_sb[:], in_=gate_ps[:])
+        for g in range(2):
+            nc.vector.quantize_mx(
+                out=wc[:, g * O : (g + 1) * O].bitcast(FP8X4),
+                scales=ws[:, g * O : (g + 1) * O],
+                in_=mu_g[:, g * 4 * O : (g + 1) * 4 * O],
+            )
+        x_quant(1)
 
         bias_bc = bias_sb[:].unsqueeze(1).to_broadcast([P, 2, O])
         outs = {}
@@ -276,14 +309,14 @@ def tile_sparsebayesianlinear_t_kernel(
             sc3 = sc[:].rearrange("p (t o) -> p t o", t=T)
             mk3 = mk[:].rearrange("p (t o) -> p t o", t=T)
 
-            d_ps = [psd.tile([P, O], F32, name="bk") for a in range(2)]
-            s_ps = [pss.tile([P, O], F32, name="bk") for a in range(2)]
             if q == 0:
-                for w, ps in ((1, s_ps), (0, d_ps)):
-                    for a in range(2):
-                        for g in range(2):
-                            mx_pass(q, a, g, w, ps[a])
+                d_ps, s_ps = d_first, s_first
+                for a in range(2):
+                    for g in range(2):
+                        mx_pass(q, a, g, 0, d_ps[a])
             else:
+                d_ps = [psd.tile([P, O], F32, name="bk") for a in range(2)]
+                s_ps = [pss.tile([P, O], F32, name="bk") for a in range(2)]
                 for a in range(2):
                     for g in range(2):
                         mx_pass(q, a, g, 1, s_ps[a])
@@ -297,6 +330,9 @@ def tile_sparsebayesianlinear_t_kernel(
             if q in FLUSH_AFTER and not fine:
                 nc.sync.dma_start(out=ov1[c][:, lo:hi, :], in_=sc3[:, lo:hi, :])
             emit_pending()
+            if q == 0:
+                nc.scalar.copy(out=bias_sb[:], in_=bias_ps[:])
+                x_copy(2)
             if 1 <= q < NPAIR - 2:
                 x_transpose(q + 2)
                 x_copy(q + 2)
@@ -319,7 +355,7 @@ def tile_sparsebayesianlinear_t_kernel(
                     adder.tensor_tensor(out=mk[:, ts], in0=mm[:, a * O : (a + 1) * O], in1=bias_sb[:], op=ALU.add)
                     nc.sync.dma_start(out=ov0[c][:, t0 + a : t0 + a + 1, :], in_=mk3[:, t0 + a : t0 + a + 1, :])
                     nc.sync.dma_start(out=ov2[c][:, t0 + a : t0 + a + 1, :], in_=mk3[:, t0 + a : t0 + a + 1, :])
-            if 1 <= q < NPAIR - 2:
+            if q + 2 < NPAIR:
                 x_quant(q + 2)
             if not fine:
                 nc.gpsimd.tensor_tensor(

@@ -15,14 +15,14 @@ P = 128
 ROWS = 4096
 K = 1024
 O = 512
-T = 4
+T = 8
 NCH = ROWS // (P * T)
 NPAIR = ROWS // (2 * P)
 NJ = O // P
 SCALE = 1.0 / 32.0
 CLAMP = 32.0
-FLUSH_AFTER = tuple(range(16))
-FINE = (NPAIR - 1,)
+SC_AFTER = (0, 1, 3, 5, 7, 9, 11, 13, 15)
+MK_AFTER = (0, 1, 2, 3, 4, 5, 7, 9, 11, 13, 15)
 
 FLOPS = 2 * 2 * ROWS * K * O
 
@@ -43,8 +43,8 @@ def tile_sparsebayesianlinear_t_kernel(
         xin = ctx.enter_context(tc.tile_pool(name="xin", bufs=1))
         xgp = ctx.enter_context(tc.tile_pool(name="xgp", bufs=3))
         xcp = ctx.enter_context(tc.tile_pool(name="xcp", bufs=4))
-        scp = ctx.enter_context(tc.tile_pool(name="scp", bufs=3))
-        mkp = ctx.enter_context(tc.tile_pool(name="mkp", bufs=3))
+        scp = ctx.enter_context(tc.tile_pool(name="scp", bufs=2))
+        mkp = ctx.enter_context(tc.tile_pool(name="mkp", bufs=2))
         ttp = ctx.enter_context(tc.tile_pool(name="ttp", bufs=2))
         mmp = ctx.enter_context(tc.tile_pool(name="mmp", bufs=2))
         psx = ctx.enter_context(tc.psum_pool(name="psx", bufs=2))
@@ -83,7 +83,10 @@ def tile_sparsebayesianlinear_t_kernel(
         x_sb = []
         for c in range(NCH):
             xt = xin.tile([P, T * K], BF16, name="x%d" % c)
-            nc.sync.dma_start(out=xt[:].rearrange("p (t k) -> p t k", t=T), in_=xv[c])
+            xt3 = xt[:].rearrange("p (t k) -> p t k", t=T)
+            step = T // 2 if c == 0 else T
+            for t in range(0, T, step):
+                nc.sync.dma_start(out=xt3[:, t : t + step, :], in_=xv[c][:, t : t + step, :])
             x_sb.append(xt)
 
         def transpose_words(src32, col0, bank):
@@ -110,11 +113,11 @@ def tile_sparsebayesianlinear_t_kernel(
         codes = {}
 
         def x_transpose(q, warm=0):
-            x32 = x_sb[q // 2][:].bitcast(F32)
+            x32 = x_sb[2 * q // T][:].bitcast(F32)
             banks = []
             for a in range(2):
                 bank = psx.tile([P, O], F32, name="bk")
-                transpose_words(x32, ((q % 2) * 2 + a) * (K // 2), bank)
+                transpose_words(x32, ((2 * q) % T + a) * (K // 2), bank)
                 banks.append(bank)
                 if warm:
                     warm_up(warm)
@@ -294,17 +297,17 @@ def tile_sparsebayesianlinear_t_kernel(
             outs["pend"] = []
 
         for q in range(NPAIR):
-            c = q // 2
-            t0 = (q % 2) * 2
+            c = 2 * q // T
+            t0 = (2 * q) % T
             if t0 == 0:
                 sc_new = scp.tile([P, T * O], F32, name="sc")
                 mk_new = mkp.tile([P, T * O], F32, name="mk")
                 outs["sc"] = sc_new
                 outs["mk"] = mk_new
-                outs["lo"] = 0
+                outs["sc_lo"] = 0
+                outs["mk_lo"] = 0
             sc = outs["sc"]
             mk = outs["mk"]
-            lo = outs["lo"]
             hi = t0 + 2
             sc3 = sc[:].rearrange("p (t o) -> p t o", t=T)
             mk3 = mk[:].rearrange("p (t o) -> p t o", t=T)
@@ -321,14 +324,13 @@ def tile_sparsebayesianlinear_t_kernel(
                     for g in range(2):
                         mx_pass(q, a, g, 1, s_ps[a])
                         mx_pass(q, a, g, 0, d_ps[a])
-            fine = q in FINE
             for a in range(2):
                 ts = slice((t0 + a) * O, (t0 + a + 1) * O)
                 nc.scalar.activation(out=sc[:, ts], in_=s_ps[a][:], func=ACT.Copy, scale=SCALE)
-                if fine:
-                    nc.sync.dma_start(out=ov1[c][:, t0 + a : t0 + a + 1, :], in_=sc3[:, t0 + a : t0 + a + 1, :])
-            if q in FLUSH_AFTER and not fine:
+            if q in SC_AFTER:
+                lo = outs["sc_lo"]
                 nc.sync.dma_start(out=ov1[c][:, lo:hi, :], in_=sc3[:, lo:hi, :])
+                outs["sc_lo"] = hi
             emit_pending()
             if q == 0:
                 nc.scalar.copy(out=bias_sb[:], in_=bias_ps[:])
@@ -339,31 +341,23 @@ def tile_sparsebayesianlinear_t_kernel(
             mm = mmp.tile([P, 2 * O], F32, name="mm")
             tts = []
             for a in range(2):
-                ts = slice((t0 + a) * O, (t0 + a + 1) * O)
                 tt = ttp.tile([P, O], F32, name="tt")
                 nc.vector.scalar_tensor_tensor(
                     out=tt[:], in0=s_ps[a][:], scalar=SCALE, in1=gate_sb[:], op0=ALU.mult, op1=ALU.subtract
                 )
                 tts.append(tt)
             for a in range(2):
-                ts = slice((t0 + a) * O, (t0 + a + 1) * O)
                 nc.vector.scalar_tensor_tensor(
                     out=mm[:, a * O : (a + 1) * O], in0=tts[a][:], scalar=0.0, in1=d_ps[a][:], op0=ALU.max, op1=ALU.mult
                 )
-                if fine:
-                    adder = nc.vector if (q == NPAIR - 1 and a == 1) else nc.gpsimd
-                    adder.tensor_tensor(out=mk[:, ts], in0=mm[:, a * O : (a + 1) * O], in1=bias_sb[:], op=ALU.add)
-                    nc.sync.dma_start(out=ov0[c][:, t0 + a : t0 + a + 1, :], in_=mk3[:, t0 + a : t0 + a + 1, :])
-                    nc.sync.dma_start(out=ov2[c][:, t0 + a : t0 + a + 1, :], in_=mk3[:, t0 + a : t0 + a + 1, :])
             if q + 2 < NPAIR:
                 x_quant(q + 2)
-            if not fine:
-                nc.gpsimd.tensor_tensor(
-                    out=mk3[:, t0:hi, :], in0=mm[:].rearrange("p (a o) -> p a o", a=2), in1=bias_bc, op=ALU.add
-                )
-            if q in FLUSH_AFTER:
-                if not fine:
-                    outs["pend"].append((ov0[c][:, lo:hi, :], mk3[:, lo:hi, :]))
-                    outs["pend"].append((ov2[c][:, lo:hi, :], mk3[:, lo:hi, :]))
-                outs["lo"] = hi
+            nc.gpsimd.tensor_tensor(
+                out=mk3[:, t0:hi, :], in0=mm[:].rearrange("p (a o) -> p a o", a=2), in1=bias_bc, op=ALU.add
+            )
+            if q in MK_AFTER:
+                lo = outs["mk_lo"]
+                outs["pend"].append((ov0[c][:, lo:hi, :], mk3[:, lo:hi, :]))
+                outs["pend"].append((ov2[c][:, lo:hi, :], mk3[:, lo:hi, :]))
+                outs["mk_lo"] = hi
         emit_pending()

@@ -21,8 +21,7 @@ NPAIR = ROWS // (2 * P)
 NJ = O // P
 SCALE = 1.0 / 32.0
 CLAMP = 32.0
-SC_AFTER = (0, 1, 3, 5, 7, 9, 11, 13, 15)
-MK_AFTER = (0, 1, 2, 3, 4, 5, 7, 9, 11, 13, 15)
+SC_AFTER = (0, 1, 2, 3, 4, 5, 7, 9, 11, 13, 14, 15)
 
 FLOPS = 2 * 2 * ROWS * K * O
 
@@ -48,8 +47,8 @@ def tile_sparsebayesianlinear_t_kernel(
         ttp = ctx.enter_context(tc.tile_pool(name="ttp", bufs=2))
         mmp = ctx.enter_context(tc.tile_pool(name="mmp", bufs=2))
         psx = ctx.enter_context(tc.psum_pool(name="psx", bufs=2))
-        pss = ctx.enter_context(tc.psum_pool(name="pss", bufs=2))
-        psd = ctx.enter_context(tc.psum_pool(name="psd", bufs=4))
+        pss = ctx.enter_context(tc.psum_pool(name="pss", bufs=3))
+        psd = ctx.enter_context(tc.psum_pool(name="psd", bufs=3))
 
         ident = const.tile([P, P], F32, name="ident")
         make_identity(nc, ident[:])
@@ -222,7 +221,7 @@ def tile_sparsebayesianlinear_t_kernel(
         excess(3)
         mu_transpose(0)
         mu_transpose(1)
-        warm_ps = psd.tile([P, O], F32, name="bk")
+        gate_ps = psd.tile([P, O], F32, name="bk")
         m2_pools = (pss, pss, psd, psd)
         for j in range(NJ):
             bank = m2_pools[j].tile([P, O], F32, name="bk")
@@ -232,13 +231,13 @@ def tile_sparsebayesianlinear_t_kernel(
                 mu_transpose(j)
         mu_copy(2, mu_banks[2])
         mu_copy(3, mu_banks[3])
-        gate_ps = psd.tile([P, O], F32, name="bk")
+        bias_ps = pss.tile([P, O], F32, name="bk")
         nc.tensor.matmul(out=gate_ps[:], lhsT=ones[:], rhs=vecs[:, 0:O], start=True, stop=True)
         x_transpose(0)
 
         def warm_up(n):
             for i in range(n):
-                nc.tensor.matmul(out=warm_ps[:], lhsT=ones[:], rhs=keys_g[:, 4 * P : 2 * 4 * P], start=True, stop=True)
+                nc.tensor.matmul(out=bias_ps[:], lhsT=ones[:], rhs=keys_g[:, 4 * P : 2 * 4 * P], start=True, stop=True)
 
         def first_scores(j):
             xc, xs = codes[0]
@@ -267,7 +266,6 @@ def tile_sparsebayesianlinear_t_kernel(
         x_quant(0)
         warm_up(2)
         x_transpose(1, 1)
-        bias_ps = psd.tile([P, O], F32, name="bk")
         nc.tensor.matmul(out=bias_ps[:], lhsT=ones[:], rhs=vecs[:, O : 2 * O], start=True, stop=True)
         d_first = [psd.tile([P, O], F32, name="bk") for a in range(2)]
         s_first = [pss.tile([P, O], F32, name="bk") for a in range(2)]
@@ -305,7 +303,6 @@ def tile_sparsebayesianlinear_t_kernel(
                 outs["sc"] = sc_new
                 outs["mk"] = mk_new
                 outs["sc_lo"] = 0
-                outs["mk_lo"] = 0
             sc = outs["sc"]
             mk = outs["mk"]
             hi = t0 + 2
@@ -355,9 +352,6 @@ def tile_sparsebayesianlinear_t_kernel(
             nc.gpsimd.tensor_tensor(
                 out=mk3[:, t0:hi, :], in0=mm[:].rearrange("p (a o) -> p a o", a=2), in1=bias_bc, op=ALU.add
             )
-            if q in MK_AFTER:
-                lo = outs["mk_lo"]
-                outs["pend"].append((ov0[c][:, lo:hi, :], mk3[:, lo:hi, :]))
-                outs["pend"].append((ov2[c][:, lo:hi, :], mk3[:, lo:hi, :]))
-                outs["mk_lo"] = hi
+            outs["pend"].append((ov0[c][:, t0:hi, :], mk3[:, t0:hi, :]))
+            outs["pend"].append((ov2[c][:, t0:hi, :], mk3[:, t0:hi, :]))
         emit_pending()

@@ -15,7 +15,7 @@ P = 128
 ROWS = 4096
 K = 1024
 O = 512
-T = 8
+T = 4
 NCH = ROWS // (P * T)
 NPAIR = ROWS // (2 * P)
 NJ = O // P
@@ -42,8 +42,8 @@ def tile_sparsebayesianlinear_t_kernel(
         xin = ctx.enter_context(tc.tile_pool(name="xin", bufs=1))
         xgp = ctx.enter_context(tc.tile_pool(name="xgp", bufs=3))
         xcp = ctx.enter_context(tc.tile_pool(name="xcp", bufs=4))
-        scp = ctx.enter_context(tc.tile_pool(name="scp", bufs=2))
-        mkp = ctx.enter_context(tc.tile_pool(name="mkp", bufs=2))
+        scp = ctx.enter_context(tc.tile_pool(name="scp", bufs=3))
+        mkp = ctx.enter_context(tc.tile_pool(name="mkp", bufs=3))
         ttp = ctx.enter_context(tc.tile_pool(name="ttp", bufs=2))
         mmp = ctx.enter_context(tc.tile_pool(name="mmp", bufs=2))
         psx = ctx.enter_context(tc.psum_pool(name="psx", bufs=2))
@@ -69,8 +69,8 @@ def tile_sparsebayesianlinear_t_kernel(
         elog = wts.tile([P, NJ * K], F32, name="elog")
         mu_g = wts.tile([P, 2 * O * 4], BF16, name="mu_g", align_bytes=64)
         keys_g = wts.tile([P, 2 * O * 4], BF16, name="keys_g", align_bytes=64)
-        wc = wts.tile([P, 2 * 2 * O], U32, name="wc", align_bytes=64)
-        ws = wts.tile([P, 2 * 2 * O], U8, name="ws", align_bytes=64)
+        wc = wts.tile([P, 2 * 2 * O], U32, name="wc", align_bytes=256)
+        ws = wts.tile([P, 2 * 2 * O], U8, name="ws", align_bytes=256)
 
         for half in range(2):
             hs = slice(half * (K // 2), (half + 1) * (K // 2))
@@ -83,9 +83,7 @@ def tile_sparsebayesianlinear_t_kernel(
         for c in range(NCH):
             xt = xin.tile([P, T * K], BF16, name="x%d" % c)
             xt3 = xt[:].rearrange("p (t k) -> p t k", t=T)
-            step = T // 2 if c == 0 else T
-            for t in range(0, T, step):
-                nc.sync.dma_start(out=xt3[:, t : t + step, :], in_=xv[c][:, t : t + step, :])
+            nc.sync.dma_start(out=xt3, in_=xv[c])
             x_sb.append(xt)
 
         def transpose_words(src32, col0, bank):
@@ -132,8 +130,8 @@ def tile_sparsebayesianlinear_t_kernel(
             xgs[q] = xg
 
         def x_quant(q):
-            xc = xcp.tile([P, 2 * 2 * P], U32, name="xc", align_bytes=64)
-            xs = xcp.tile([P, 2 * 2 * P], U8, name="xs", align_bytes=64)
+            xc = xcp.tile([P, 2 * 2 * P], U32, name="xc", align_bytes=256)
+            xs = xcp.tile([P, 2 * 2 * P], U8, name="xs", align_bytes=256)
             nc.vector.quantize_mx(out=xc[:].bitcast(FP8X4), scales=xs[:], in_=xgs[q][:])
             codes[q] = (xc, xs)
 

@@ -347,9 +347,15 @@ def tile_sparsebayesianlinear_t_kernel(
                 )
             if q + 2 < NPAIR:
                 x_quant(q + 2)
-            nc.gpsimd.tensor_tensor(
-                out=mk3[:, t0:hi, :], in0=mm[:].rearrange("p (a o) -> p a o", a=2), in1=bias_bc, op=ALU.add
-            )
+            if q < NPAIR - 1:
+                nc.gpsimd.tensor_tensor(
+                    out=mk3[:, t0:hi, :], in0=mm[:].rearrange("p (a o) -> p a o", a=2), in1=bias_bc, op=ALU.add
+                )
+            else:
+                for a in range(2):
+                    nc.vector.tensor_tensor(
+                        out=mk3[:, t0 + a, :], in0=mm[:, a * O : (a + 1) * O], in1=bias_sb[:], op=ALU.add
+                    )
             outs["pend"].append((ov0[c][:, t0:hi, :], mk3[:, t0:hi, :]))
             outs["pend"].append((ov2[c][:, t0:hi, :], mk3[:, t0:hi, :]))
         emit_pending()

from contextlib import ExitStack

import concourse.mybir as mybir
from concourse.masks import make_identity

F32 = mybir.dt.float32
BF16 = mybir.dt.bfloat16
U32 = mybir.dt.uint32
U8 = mybir.dt.uint8
FP8X4 = mybir.dt.float8_e4m3fn_x4
ALU = mybir.AluOpType
ACT = mybir.ActivationFunctionType

P = 128
ROWS = 4096
K = 1024
O = 512
T = 4
NCH = ROWS // (P * T)
NPAIR = ROWS // (2 * P)
NJ = O // P
SCALE = 1.0 / 32.0
CLAMP = 32.0
SC_AFTER = (0, 1, 2, 3, 4, 5, 7, 9, 11, 13, 14, 15)

FLOPS = 2 * 2 * ROWS * K * O


def tile_sparsebayesianlinear_t_kernel(
    tc, x, mu_weight, sigma_weight, gate_param, mu_bias, out_0, out_1, out_2
):
    nc = tc.nc
    xv = x.flatten_outer_dims().rearrange("(c p t) k -> c p t k", c=NCH, p=P)
    ov0 = out_0.flatten_outer_dims().rearrange("(c p t) o -> c p t o", c=NCH, p=P)
    ov1 = out_1.rearrange("(c p t) o -> c p t o", c=NCH, p=P)
    ov2 = out_2.rearrange("(c p t) o -> c p t o", c=NCH, p=P)

    with ExitStack() as ctx:
        ctx.enter_context(tc.manual_schedule())
        const = ctx.enter_context(tc.tile_pool(name="const", bufs=1))
        wts = ctx.enter_context(tc.tile_pool(name="wts", bufs=1))
        xin = ctx.enter_context(tc.tile_pool(name="xin", bufs=1))
        xgp = ctx.enter_context(tc.tile_pool(name="xgp", bufs=3))
        xcp = ctx.enter_context(tc.tile_pool(name="xcp", bufs=4))
        scp = ctx.enter_context(tc.tile_pool(name="scp", bufs=3))
        mkp = ctx.enter_context(tc.tile_pool(name="mkp", bufs=3))
        ttp = ctx.enter_context(tc.tile_pool(name="ttp", bufs=2))
        mmp = ctx.enter_context(tc.tile_pool(name="mmp", bufs=2))
        psx = ctx.enter_context(tc.psum_pool(name="psx", bufs=2))
        pss = ctx.enter_context(tc.psum_pool(name="pss", bufs=3))
        psd = ctx.enter_context(tc.psum_pool(name="psd", bufs=3))

        ident = const.tile([P, P], F32, name="ident")
        make_identity(nc, ident[:])
        ones = const.tile([P, P], BF16, name="ones")
        nc.vector.memset(ones[:], 1.0)
        vecs = const.tile([P, 2 * O], BF16, name="vecs")
        nc.vector.memset(vecs[:].bitcast(U32), 0)
        warm = const.tile([P, 1], F32, name="warm")
        nc.scalar.activation(out=warm[:], in_=ones[:, 0:1], func=ACT.Exp)
        nc.scalar.dma_start(out=vecs[0:1, 0:O], in_=gate_param.unsqueeze(0))
        nc.scalar.dma_start(out=vecs[0:1, O : 2 * O], in_=mu_bias.unsqueeze(0))
        bias_sb = const.tile([P, O], F32, name="bias_sb")
        gate_sb = const.tile([P, O], F32, name="gate_sb")

        sig = wts.tile([P, NJ * K], BF16, name="sig")
        mur = wts.tile([P, NJ * K], BF16, name="mur")
        vcl = wts.tile([P, NJ * K], BF16, name="vcl")
        elog = wts.tile([P, NJ * K], F32, name="elog")
        mu_g = wts.tile([P, 2 * O * 4], BF16, name="mu_g", align_bytes=64)
        keys_g = wts.tile([P, 2 * O * 4], BF16, name="keys_g", align_bytes=64)
        wc = wts.tile([P, 2 * 2 * O], U32, name="wc", align_bytes=256)
        ws = wts.tile([P, 2 * 2 * O], U8, name="ws", align_bytes=256)

        for half in range(2):
            hs = slice(half * (K // 2), (half + 1) * (K // 2))
            nc.sync.dma_start(out=sig[:, hs], in_=sigma_weight[0:P, hs])
        for j in range(1, NJ):
            nc.sync.dma_start(out=sig[:, j * K : (j + 1) * K], in_=sigma_weight[j * P : (j + 1) * P, :])
        for j in range(NJ):
            nc.sync.dma_start(out=mur[:, j * K : (j + 1) * K], in_=mu_weight[j * P : (j + 1) * P, :])
        x_sb = []
        for c in range(NCH):
            xt = xin.tile([P, T * K], BF16, name="x%d" % c)
            xt3 = xt[:].rearrange("p (t k) -> p t k", t=T)
            nc.sync.dma_start(out=xt3, in_=xv[c])
            x_sb.append(xt)

        def transpose_words(src32, col0, bank):
            for i in range(4):
                nc.tensor.transpose(
                    out=bank[:, i * P : (i + 1) * P],
                    in_=src32[:, col0 + i * P : col0 + (i + 1) * P],
                    identity=ident[:],
                )

        vcl32 = vcl[:].bitcast(F32)
        sig32 = sig[:].bitcast(F32)
        mur32 = mur[:].bitcast(F32)
        mu_g32 = mu_g[:].bitcast(F32).rearrange("p (g o u) -> p g o u", g=2, u=2)

        def mu_copy(j, bank):
            nc.vector.tensor_copy(
                out=mu_g32[:, :, j * P : (j + 1) * P, :],
                in_=bank[:].rearrange("p (g u r) -> p g r u", g=2, u=2),
            )

        xbanks = {}
        xgs = {}
        codes = {}

        def x_transpose(q, warm=0):
            x32 = x_sb[2 * q // T][:].bitcast(F32)
            banks = []
            for a in range(2):
                bank = psx.tile([P, O], F32, name="bk")
                transpose_words(x32, ((2 * q) % T + a) * (K // 2), bank)
                banks.append(bank)
                if warm:
                    warm_up(warm)
            xbanks[q] = banks

        def x_copy(q):
            xg = xgp.tile([P, 2 * K], BF16, name="xg", align_bytes=64)
            xg32 = xg[:].bitcast(F32).rearrange("p (a g r u) -> p a g r u", a=2, g=2, u=2)
            for a in range(2):
                nc.scalar.copy(
                    out=xg32[:, a], in_=xbanks[q][a][:].rearrange("p (g u r) -> p g r u", g=2, u=2)
                )
            xgs[q] = xg

        def x_quant(q):
            xc = xcp.tile([P, 2 * 2 * P], U32, name="xc", align_bytes=256)
            xs = xcp.tile([P, 2 * 2 * P], U8, name="xs", align_bytes=256)
            nc.vector.quantize_mx(out=xc[:].bitcast(FP8X4), scales=xs[:], in_=xgs[q][:])
            codes[q] = (xc, xs)

        def mx_pass(q, a, g, w, ps):
            xc, xs = codes[q]
            l0 = a * 2 * P + g * P
            w0 = w * 2 * O + g * O
            nc.tensor.matmul_mx(
                out=ps[:],
                lhsT=xc[:, l0 : l0 + P].bitcast(FP8X4),
                lhsT_scale=xs[:, l0 : l0 + P],
                rhs=wc[:, w0 : w0 + O].bitcast(FP8X4),
                rhs_scale=ws[:, w0 : w0 + O],
                start=(g == 0),
                stop=(g == 1),
            )

        def softplus_exp(j, bank, part, parts):
            width = K // parts
            cs = slice(j * K + part * width, j * K + (part + 1) * width)
            nc.vector.tensor_scalar_min(out=vcl[:, cs], in0=sig[:, cs], scalar1=CLAMP)
            for b in range(width // (2 * P)):
                w = cs.start // 2 + b * P
                nc.tensor.transpose(out=bank[:, b * P : (b + 1) * P], in_=vcl32[:, w : w + P], identity=ident[:])
            nc.scalar.activation(out=elog[:, cs], in_=bank[:].bitcast(BF16)[:, 0:width], func=ACT.Exp)

        def excess(j):
            js = slice(j * K, (j + 1) * K)
            nc.vector.tensor_scalar(
                out=sig[:, js], in0=sig[:, js], scalar1=1.0 / CLAMP, scalar2=1.0, op0=ALU.mult, op1=ALU.max
            )

        mu_banks = {}
        m2_banks = {}

        def mu_transpose(j):
            bank = psx.tile([P, O], F32, name="bk")
            transpose_words(mur32, j * (K // 2), bank)
            mu_banks[j] = bank

        def m2_make(j, bank):
            js = slice(j * K, (j + 1) * K)
            nc.vector.tensor_tensor(out=sig[:, js], in0=sig[:, js], in1=mur[:, js], op=ALU.mult)
            transpose_words(sig32, j * (K // 2), bank)
            m2_banks[j] = bank

        def keys_mult(j):
            m2v = m2_banks[j][:].bitcast(BF16)
            for g in range(2):
                nc.vector.tensor_tensor(
                    out=keys_g[:, g * 4 * O + j * 4 * P : g * 4 * O + (j + 1) * 4 * P].rearrange(
                        "p (r u e) -> p r u e", u=2, e=2
                    ),
                    in0=elog[:, j * K + g * 512 : j * K + (g + 1) * 512].rearrange(
                        "p (u r e) -> p r u e", u=2, e=2
                    ),
                    in1=m2v[:, g * 512 : (g + 1) * 512].rearrange("p (u r e) -> p r u e", u=2, e=2),
                    op=ALU.mult,
                )

        def keys_quant(j):
            for g in range(2):
                w0 = 2 * O + g * O + j * P
                nc.vector.quantize_mx(
                    out=wc[:, w0 : w0 + P].bitcast(FP8X4),
                    scales=ws[:, w0 : w0 + P],
                    in_=keys_g[:, g * 4 * O + j * 4 * P : g * 4 * O + (j + 1) * 4 * P],
                )

        def log_part(j, g):
            gs = slice(j * K + g * 512, j * K + (g + 1) * 512)
            nc.scalar.activation(out=elog[:, gs], in_=elog[:, gs], func=ACT.Ln, bias=1.0)

        v_pools = (pss, pss, psd, psd)
        v_half = psx.tile([P, O], F32, name="bk")
        v_banks = [v_pools[j].tile([P, O], F32, name="bk") for j in range(NJ)]
        softplus_exp(0, v_half, 0, 2)
        softplus_exp(0, v_banks[0], 1, 2)
        softplus_exp(1, v_banks[1], 0, 1)
        excess(0)
        softplus_exp(2, v_banks[2], 0, 1)
        excess(1)
        softplus_exp(3, v_banks[3], 0, 1)
        excess(2)
        excess(3)
        mu_transpose(0)
        mu_transpose(1)
        gate_ps = psd.tile([P, O], F32, name="bk")
        m2_pools = (pss, pss, psd, psd)
        for j in range(NJ):
            bank = m2_pools[j].tile([P, O], F32, name="bk")
            m2_make(j, bank)
            if j >= 2:
                mu_copy(j - 2, mu_banks[j - 2])
                mu_transpose(j)
        mu_copy(2, mu_banks[2])
        mu_copy(3, mu_banks[3])
        bias_ps = pss.tile([P, O], F32, name="bk")
        nc.tensor.matmul(out=gate_ps[:], lhsT=ones[:], rhs=vecs[:, 0:O], start=True, stop=True)
        x_transpose(0)

        def warm_up(n):
            for i in range(n):
                nc.tensor.matmul(out=bias_ps[:], lhsT=ones[:], rhs=keys_g[:, 4 * P : 2 * 4 * P], start=True, stop=True)

        def first_scores(j):
            xc, xs = codes[0]
            for a in range(2):
                for g in range(2):
                    l0 = a * 2 * P + g * P
                    w0 = 2 * O + g * O + j * P
                    nc.tensor.matmul_mx(
                        out=s_first[a][:, j * P : (j + 1) * P],
                        lhsT=xc[:, l0 : l0 + P].bitcast(FP8X4),
                        lhsT_scale=xs[:, l0 : l0 + P],
                        rhs=wc[:, w0 : w0 + P].bitcast(FP8X4),
                        rhs_scale=ws[:, w0 : w0 + P],
                        start=(g == 0),
                        stop=(g == 1),
                    )

        for j in range(NJ - 1):
            log_part(j, 0)
            log_part(j, 1)
            keys_mult(j)
            keys_quant(j)
        x_copy(0)
        log_part(NJ - 1, 0)
        log_part(NJ - 1, 1)
        x_quant(0)
        warm_up(2)
        x_transpose(1, 1)
        nc.tensor.matmul(out=bias_ps[:], lhsT=ones[:], rhs=vecs[:, O : 2 * O], start=True, stop=True)
        d_first = [psd.tile([P, O], F32, name="bk") for a in range(2)]
        s_first = [pss.tile([P, O], F32, name="bk") for a in range(2)]
        keys_mult(NJ - 1)
        for j in range(NJ - 1):
            first_scores(j)
        keys_quant(NJ - 1)
        first_scores(NJ - 1)
        x_copy(1)
        x_transpose(2)
        nc.scalar.copy(out=gate_sb[:], in_=gate_ps[:])
        for g in range(2):
            nc.vector.quantize_mx(
                out=wc[:, g * O : (g + 1) * O].bitcast(FP8X4),
                scales=ws[:, g * O : (g + 1) * O],
                in_=mu_g[:, g * 4 * O : (g + 1) * 4 * O],
            )
        x_quant(1)

        bias_bc = bias_sb[:].unsqueeze(1).to_broadcast([P, 2, O])
        outs = {}
        outs["pend"] = []

        def emit_pending():
            for dst, src_ap in outs["pend"]:
                nc.sync.dma_start(out=dst, in_=src_ap)
            outs["pend"] = []

        for q in range(NPAIR):
            c = 2 * q // T
            t0 = (2 * q) % T
            if t0 == 0:
                sc_new = scp.tile([P, T * O], F32, name="sc")
                mk_new = mkp.tile([P, T * O], F32, name="mk")
                outs["sc"] = sc_new
                outs["mk"] = mk_new
                outs["sc_lo"] = 0
            sc = outs["sc"]
            mk = outs["mk"]
            hi = t0 + 2
            sc3 = sc[:].rearrange("p (t o) -> p t o", t=T)
            mk3 = mk[:].rearrange("p (t o) -> p t o", t=T)

            if q == 0:
                d_ps, s_ps = d_first, s_first
                for a in range(2):
                    for g in range(2):
                        mx_pass(q, a, g, 0, d_ps[a])
            else:
                d_ps = [psd.tile([P, O], F32, name="bk") for a in range(2)]
                s_ps = [pss.tile([P, O], F32, name="bk") for a in range(2)]
                for a in range(2):
                    for g in range(2):
                        mx_pass(q, a, g, 1, s_ps[a])
                        mx_pass(q, a, g, 0, d_ps[a])
            for a in range(2):
                ts = slice((t0 + a) * O, (t0 + a + 1) * O)
                nc.scalar.activation(out=sc[:, ts], in_=s_ps[a][:], func=ACT.Copy, scale=SCALE)
            if q in SC_AFTER:
                lo = outs["sc_lo"]
                nc.sync.dma_start(out=ov1[c][:, lo:hi, :], in_=sc3[:, lo:hi, :])
                outs["sc_lo"] = hi
            emit_pending()
            if q == 0:
                nc.scalar.copy(out=bias_sb[:], in_=bias_ps[:])
                x_copy(2)
            if 1 <= q < NPAIR - 2:
                x_transpose(q + 2)
                x_copy(q + 2)
            mm = mmp.tile([P, 2 * O], F32, name="mm")
            tts = []
            for a in range(2):
                tt = ttp.tile([P, O], F32, name="tt")
                nc.vector.scalar_tensor_tensor(
                    out=tt[:], in0=s_ps[a][:], scalar=SCALE, in1=gate_sb[:], op0=ALU.mult, op1=ALU.subtract
                )
                tts.append(tt)
            for a in range(2):
                nc.vector.scalar_tensor_tensor(
                    out=mm[:, a * O : (a + 1) * O], in0=tts[a][:], scalar=0.0, in1=d_ps[a][:], op0=ALU.max, op1=ALU.mult
                )
            if q + 2 < NPAIR:
                x_quant(q + 2)
            if q < NPAIR - 1:
                nc.gpsimd.tensor_tensor(
                    out=mk3[:, t0:hi, :], in0=mm[:].rearrange("p (a o) -> p a o", a=2), in1=bias_bc, op=ALU.add
                )
            else:
                for a in range(2):
                    nc.vector.tensor_tensor(
                        out=mk3[:, t0 + a, :], in0=mm[:, a * O : (a + 1) * O], in1=bias_sb[:], op=ALU.add
                    )
            outs["pend"].append((ov0[c][:, t0:hi, :], mk3[:, t0:hi, :]))
            outs["pend"].append((ov2[c][:, t0:hi, :], mk3[:, t0:hi, :]))
        emit_pending()
